import numpy as np
import ml_dtypes


def mxq(x, axis, fmt="e4m3"):
    dtype, down = {"e4m3": (ml_dtypes.float8_e4m3fn, 7), "e5m2": (ml_dtypes.float8_e5m2, 14)}[fmt]
    v = np.moveaxis(np.asarray(x, np.float32).astype(ml_dtypes.bfloat16).astype(np.float64), axis, -1)
    blocks = v.reshape(v.shape[:-1] + (-1, 32))
    amax = np.abs(blocks).max(-1, keepdims=True)
    byte = np.maximum(np.where(amax > 0, np.frexp(amax)[1] - 1 + 127, 0) - down, 1)
    scale = np.exp2(byte - 127.0)
    codes = (blocks / scale).astype(np.float32).astype(dtype).astype(np.float64)
    return np.moveaxis((codes * scale).reshape(v.shape), -1, axis)


WIDE = False


def mx_kscale(k):
    if not WIDE:
        return np.ones(k)
    levels = np.array([10, -10, 5, -5, 0])
    a = np.random.permutation(np.resize(levels, k // 512 * 4)).reshape(k // 512, 4)
    idx = np.arange(k)
    return np.exp2(a[idx // 512, idx % 128 // 32])


BF16 = ml_dtypes.bfloat16


def bf(x):
    return np.asarray(x, np.float32).astype(BF16)


def f64(x):
    return np.asarray(x).astype(np.float64)


B, N, J = 64, 512, 32
DECAY = 0.8


def decay_pattern(n, decay):
    i = np.arange(n)[:, None]
    j = np.arange(n)[None, :]
    w = np.where(j <= i, decay ** (1.0 * np.maximum(i - j, 0)), 0.0)
    return w / w.sum(axis=1, keepdims=True)


def setup_inputs():
    s = mx_kscale(N)
    x = np.random.standard_normal((B, N, J)) * (np.sqrt(N) / 8.0) * s.mean() / s[None, :, None]
    off = 1.5 * np.random.standard_normal((J, N, N)) + np.log(s)[None, None, :]
    pre = 8.0 * decay_pattern(N, DECAY) + 0.2 * np.random.standard_normal((N, N))
    return {"x": bf(x), "learnable_offset": bf(off), "predefined_weights": bf(pre)}


def reference(x, learnable_offset, predefined_weights):
    z = f64(predefined_weights)[None, :, :] + f64(learnable_offset)
    e = np.exp(z - z.max(-1, keepdims=True))
    masks = e / e.sum(-1, keepdims=True)
    y = mxq(f64(x), 1, "e4m3").transpose(2, 0, 1) @ mxq(masks, 2, "e4m3").transpose(0, 2, 1)
    return y.transpose(1, 2, 0)

@@ -1,0 +1,131 @@
+from contextlib import ExitStack
+
+import concourse.mybir as mybir
+from concourse.masks import make_identity
+
+FLOPS = 2 * 64 * 512 * 512 * 32
+
+BF16 = mybir.dt.bfloat16
+F32 = mybir.dt.float32
+U32 = mybir.dt.uint32
+U8 = mybir.dt.uint8
+FP8X4 = mybir.dt.float8_e4m3fn_x4
+ALU = mybir.AluOpType
+ACT = mybir.ActivationFunctionType
+AX = mybir.AxisListType
+
+P = 128
+B, N, J = 64, 512, 32
+NT = N // P
+PACK = 4
+JU = 4
+NORM_ON_SCALAR = (1, 3)
+
+
+def tile_learnablemasktemporalaggregation_kernel(tc, x, learnable_offset, predefined_weights, out):
+    nc = tc.nc
+    off_v = learnable_offset.rearrange("j (a p) m -> a p j m", p=P)
+    pre_v = predefined_weights.rearrange("(a p) m -> p a m", p=P)
+    x_v = x.rearrange("b (t p) j -> p (b t) j", p=P)
+    out_v = out.rearrange("b (a p) j -> a p b j", p=P)
+
+    with ExitStack() as ctx:
+        const = ctx.enter_context(tc.tile_pool(name="const", bufs=1))
+        ld = ctx.enter_context(tc.tile_pool(name="ld", bufs=4))
+        zp = ctx.enter_context(tc.tile_pool(name="zp", bufs=4))
+        st = ctx.enter_context(tc.tile_pool(name="st", bufs=6))
+        mp = ctx.enter_context(tc.tile_pool(name="mp", bufs=3))
+        gp = ctx.enter_context(tc.tile_pool(name="gp", bufs=3))
+        cp = ctx.enter_context(tc.tile_pool(name="cp", bufs=8))
+        op = ctx.enter_context(tc.tile_pool(name="op", bufs=2))
+        psum_t = ctx.enter_context(tc.psum_pool(name="psum_t", bufs=4))
+        psum_o = ctx.enter_context(tc.psum_pool(name="psum_o", bufs=2))
+
+        pre_sb = const.tile([P, NT, N], BF16)
+        nc.sync.dma_start(out=pre_sb[:], in_=pre_v)
+        x_raw = const.tile([P, B * PACK, J], BF16)
+        for c in range(4):
+            nc.gpsimd.dma_start(out=x_raw[:, 64 * c:64 * (c + 1), :], in_=x_v[:, 64 * c:64 * (c + 1), :])
+        ident = const.tile([P, P], BF16)
+        make_identity(nc, ident[:])
+
+        x_grp = const.tile([P, J, B * PACK], BF16, align_bytes=64)
+        x_codes = const.tile([P, J * B], U32, align_bytes=64)
+        x_scl = const.tile([P, J * B], U8, align_bytes=64)
+        for g in range(J // 8):
+            nc.gpsimd.tensor_scalar(
+                out=x_grp[:, 8 * g:8 * (g + 1), :],
+                in0=x_raw[:, :, 8 * g:8 * (g + 1)].rearrange("p c j -> p j c"),
+                scalar1=1.0, scalar2=0.0, op0=ALU.mult, op1=ALU.add,
+            )
+            nc.vector.quantize_mx(
+                out=x_codes[:, 512 * g:512 * (g + 1)].bitcast(FP8X4),
+                scales=x_scl[:, 512 * g:512 * (g + 1)],
+                in_=x_grp[:, 8 * g:8 * (g + 1), :].rearrange("p j c -> p (j c)"),
+            )
+
+        for a in range(NT):
+            o_sb = op.tile([P, B, J], F32)
+            for g in range(J // 8):
+                po = psum_o.tile([P, 8, B], F32)
+                for h in range(2):
+                    j0 = 8 * g + JU * h
+                    off_sb = ld.tile([P, JU, N], BF16)
+                    nc.sync.dma_start(out=off_sb[:], in_=off_v[a][:, j0:j0 + JU, :])
+                    z = zp.tile([P, JU, N], F32)
+                    nc.vector.tensor_tensor(
+                        out=z[:], in0=off_sb[:],
+                        in1=pre_sb[:, a:a + 1, :].to_broadcast([P, JU, N]), op=ALU.add,
+                    )
+                    negmax = st.tile([P, JU], F32)
+                    nc.vector.tensor_reduce(out=negmax[:], in_=z[:], axis=AX.X, op=ALU.max, negate=True)
+                    ssum = st.tile([P, JU], F32)
+                    for jj in range(JU):
+                        nc.scalar.activation(
+                            out=z[:, jj, :], in_=z[:, jj, :], func=ACT.Exp,
+                            bias=negmax[:, jj:jj + 1], scale=1.0, accum_out=ssum[:, jj:jj + 1],
+                        )
+                    rinv = st.tile([P, JU], F32)
+                    nc.vector.reciprocal(out=rinv[:], in_=ssum[:])
+                    mask = mp.tile([P, JU, N], BF16)
+                    for jj in range(JU):
+                        if jj in NORM_ON_SCALAR:
+                            nc.scalar.activation(
+                                out=mask[:, jj, :], in_=z[:, jj, :], func=ACT.Copy, scale=rinv[:, jj:jj + 1],
+                            )
+                        else:
+                            nc.vector.tensor_scalar(
+                                out=mask[:, jj, :], in0=z[:, jj, :], scalar1=rinv[:, jj:jj + 1],
+                                scalar2=None, op0=ALU.mult,
+                            )
+                    grp = gp.tile([P, JU, P, PACK], BF16, align_bytes=64)
+                    for half in range(2):
+                        pt = psum_t.tile([P, 2, PACK, P], BF16)
+                        for q in range(2):
+                            jj = 2 * half + q
+                            for t in range(PACK):
+                                nc.tensor.transpose(pt[:, q, t, :], mask[:, jj, t * P:(t + 1) * P], ident[:])
+                        nc.scalar.copy(
+                            out=grp[:, 2 * half:2 * half + 2, :, :],
+                            in_=pt[:].rearrange("p q t n -> p q n t"),
+                        )
+                    codes = cp.tile([P, JU * P], U32, align_bytes=64)
+                    scl = cp.tile([P, JU * P], U8, align_bytes=64)
+                    nc.vector.quantize_mx(
+                        out=codes[:].bitcast(FP8X4), scales=scl[:],
+                        in_=grp[:].rearrange("p j n t -> p (j n t)"),
+                    )
+                    for jj in range(JU):
+                        j = j0 + jj
+                        nc.tensor.matmul_mx(
+                            out=po[:, JU * h + jj, :],
+                            lhsT=codes[:, jj * P:(jj + 1) * P].bitcast(FP8X4),
+                            lhsT_scale=scl[:, jj * P:(jj + 1) * P],
+                            rhs=x_codes[:, j * B:(j + 1) * B].bitcast(FP8X4),
+                            rhs_scale=x_scl[:, j * B:(j + 1) * B],
+                            start=True, stop=True,
+                        )
+                nc.vector.tensor_copy(
+                    out=o_sb[:, :, 8 * g:8 * (g + 1)], in_=po[:].rearrange("p j b -> p b j"),
+                )
+            nc.sync.dma_start(out=out_v[a], in_=o_sb[:])

@@ -19,7 +19,20 @@ B, N, J = 64, 512, 32
 NT = N // P
 PACK = 4
 JU = 4
-NORM_ON_SCALAR = (1, 3)
+UNITS = [(a, j0) for a in range(NT) for j0 in range(0, J, JU)]
+NU = len(UNITS)
+UPA = J // JU
+
+LAG_E = 1
+LAG_R = 1
+LAG_N = 2
+LAG_T = 2
+LAG_C = 3
+LAG_Q = 4
+LAG_MX = 10
+LAG_EV = 11
+X_STEP = 7
+PREFETCH = 3
 
 
 def tile_learnablemasktemporalaggregation_kernel(tc, x, learnable_offset, predefined_weights, out):
@@ -31,15 +44,20 @@ def tile_learnablemasktemporalaggregation_kernel(tc, x, learnable_offset, predef
 
     with ExitStack() as ctx:
         const = ctx.enter_context(tc.tile_pool(name="const", bufs=1))
-        ld = ctx.enter_context(tc.tile_pool(name="ld", bufs=4))
+        ld = ctx.enter_context(tc.tile_pool(name="ld", bufs=PREFETCH + 1))
         zp = ctx.enter_context(tc.tile_pool(name="zp", bufs=4))
         st = ctx.enter_context(tc.tile_pool(name="st", bufs=6))
         mp = ctx.enter_context(tc.tile_pool(name="mp", bufs=3))
         gp = ctx.enter_context(tc.tile_pool(name="gp", bufs=3))
-        cp = ctx.enter_context(tc.tile_pool(name="cp", bufs=8))
+        cp = ctx.enter_context(tc.tile_pool(name="cp", bufs=LAG_MX - LAG_Q + 2))
         op = ctx.enter_context(tc.tile_pool(name="op", bufs=2))
+        psum_c = ctx.enter_context(tc.psum_pool(name="psum_c", bufs=1))
         psum_t = ctx.enter_context(tc.psum_pool(name="psum_t", bufs=4))
         psum_o = ctx.enter_context(tc.psum_pool(name="psum_o", bufs=2))
+        ctx.enter_context(tc.manual_schedule())
+
+        off_t, z_t, nmax_t, ssum_t, rinv_t, mask_t = {}, {}, {}, {}, {}, {}
+        pt_t, grp_t, codes_t, scl_t, po_t, o_t = {}, {}, {}, {}, {}, {}
 
         pre_sb = const.tile([P, NT, N], BF16)
         nc.sync.dma_start(out=pre_sb[:], in_=pre_v)
@@ -48,84 +66,144 @@ def tile_learnablemasktemporalaggregation_kernel(tc, x, learnable_offset, predef
             nc.gpsimd.dma_start(out=x_raw[:, 64 * c:64 * (c + 1), :], in_=x_v[:, 64 * c:64 * (c + 1), :])
         ident = const.tile([P, P], BF16)
         make_identity(nc, ident[:])
+        pre_ps = [psum_c.tile([P, 2, N], BF16, name="pre_ps%d" % i) for i in range(2)]
+        for a in range(NT):
+            nc.tensor.matmul(out=pre_ps[a // 2][:, a % 2, :], lhsT=ident[:], rhs=pre_sb[:, a, :], start=True, stop=True)
 
         x_grp = const.tile([P, J, B * PACK], BF16, align_bytes=64)
         x_codes = const.tile([P, J * B], U32, align_bytes=64)
         x_scl = const.tile([P, J * B], U8, align_bytes=64)
-        for g in range(J // 8):
+
+        def x_group(c):
             nc.gpsimd.tensor_scalar(
-                out=x_grp[:, 8 * g:8 * (g + 1), :],
-                in0=x_raw[:, :, 8 * g:8 * (g + 1)].rearrange("p c j -> p j c"),
+                out=x_grp[:, JU * c:JU * (c + 1), :],
+                in0=x_raw[:, :, JU * c:JU * (c + 1)].rearrange("p c j -> p j c"),
                 scalar1=1.0, scalar2=0.0, op0=ALU.mult, op1=ALU.add,
             )
+
+        def x_quant(c):
+            w = JU * B
             nc.vector.quantize_mx(
-                out=x_codes[:, 512 * g:512 * (g + 1)].bitcast(FP8X4),
-                scales=x_scl[:, 512 * g:512 * (g + 1)],
-                in_=x_grp[:, 8 * g:8 * (g + 1), :].rearrange("p j c -> p (j c)"),
+                out=x_codes[:, w * c:w * (c + 1)].bitcast(FP8X4),
+                scales=x_scl[:, w * c:w * (c + 1)],
+                in_=x_grp[:, JU * c:JU * (c + 1), :].rearrange("p j c -> p (j c)"),
             )
 
-        for a in range(NT):
-            o_sb = op.tile([P, B, J], F32)
-            for g in range(J // 8):
-                po = psum_o.tile([P, 8, B], F32)
-                for h in range(2):
-                    j0 = 8 * g + JU * h
-                    off_sb = ld.tile([P, JU, N], BF16)
-                    nc.sync.dma_start(out=off_sb[:], in_=off_v[a][:, j0:j0 + JU, :])
-                    z = zp.tile([P, JU, N], F32)
-                    nc.vector.tensor_tensor(
-                        out=z[:], in0=off_sb[:],
-                        in1=pre_sb[:, a:a + 1, :].to_broadcast([P, JU, N]), op=ALU.add,
-                    )
-                    negmax = st.tile([P, JU], F32)
-                    nc.vector.tensor_reduce(out=negmax[:], in_=z[:], axis=AX.X, op=ALU.max, negate=True)
-                    ssum = st.tile([P, JU], F32)
-                    for jj in range(JU):
-                        nc.scalar.activation(
-                            out=z[:, jj, :], in_=z[:, jj, :], func=ACT.Exp,
-                            bias=negmax[:, jj:jj + 1], scale=1.0, accum_out=ssum[:, jj:jj + 1],
-                        )
-                    rinv = st.tile([P, JU], F32)
-                    nc.vector.reciprocal(out=rinv[:], in_=ssum[:])
-                    mask = mp.tile([P, JU, N], BF16)
-                    for jj in range(JU):
-                        if jj in NORM_ON_SCALAR:
-                            nc.scalar.activation(
-                                out=mask[:, jj, :], in_=z[:, jj, :], func=ACT.Copy, scale=rinv[:, jj:jj + 1],
-                            )
-                        else:
-                            nc.vector.tensor_scalar(
-                                out=mask[:, jj, :], in0=z[:, jj, :], scalar1=rinv[:, jj:jj + 1],
-                                scalar2=None, op0=ALU.mult,
-                            )
-                    grp = gp.tile([P, JU, P, PACK], BF16, align_bytes=64)
-                    for half in range(2):
-                        pt = psum_t.tile([P, 2, PACK, P], BF16)
-                        for q in range(2):
-                            jj = 2 * half + q
-                            for t in range(PACK):
-                                nc.tensor.transpose(pt[:, q, t, :], mask[:, jj, t * P:(t + 1) * P], ident[:])
-                        nc.scalar.copy(
-                            out=grp[:, 2 * half:2 * half + 2, :, :],
-                            in_=pt[:].rearrange("p q t n -> p q n t"),
-                        )
-                    codes = cp.tile([P, JU * P], U32, align_bytes=64)
-                    scl = cp.tile([P, JU * P], U8, align_bytes=64)
-                    nc.vector.quantize_mx(
-                        out=codes[:].bitcast(FP8X4), scales=scl[:],
-                        in_=grp[:].rearrange("p j n t -> p (j n t)"),
-                    )
-                    for jj in range(JU):
-                        j = j0 + jj
-                        nc.tensor.matmul_mx(
-                            out=po[:, JU * h + jj, :],
-                            lhsT=codes[:, jj * P:(jj + 1) * P].bitcast(FP8X4),
-                            lhsT_scale=scl[:, jj * P:(jj + 1) * P],
-                            rhs=x_codes[:, j * B:(j + 1) * B].bitcast(FP8X4),
-                            rhs_scale=x_scl[:, j * B:(j + 1) * B],
-                            start=True, stop=True,
-                        )
-                nc.vector.tensor_copy(
-                    out=o_sb[:, :, 8 * g:8 * (g + 1)], in_=po[:].rearrange("p j b -> p b j"),
+        def load(u):
+            a, j0 = UNITS[u]
+            off_t[u] = ld.tile([P, JU, N], BF16, name="off")
+            nc.sync.dma_start(out=off_t[u][:], in_=off_v[a][:, j0:j0 + JU, :])
+
+        def add_max(u):
+            a, j0 = UNITS[u]
+            z_t[u] = zp.tile([P, JU, N], F32, name="z")
+            nc.vector.tensor_tensor(
+                out=z_t[u][:], in0=off_t[u][:],
+                in1=pre_ps[a // 2][:, a % 2:a % 2 + 1, :].to_broadcast([P, JU, N]), op=ALU.add,
+            )
+            nmax_t[u] = st.tile([P, JU], F32, name="nmax")
+            nc.vector.tensor_reduce(out=nmax_t[u][:], in_=z_t[u][:], axis=AX.X, op=ALU.max, negate=True)
+
+        def exps(u):
+            ssum_t[u] = st.tile([P, JU], F32, name="ssum")
+            for jj in range(JU):
+                nc.scalar.activation(
+                    out=z_t[u][:, jj, :], in_=z_t[u][:, jj, :], func=ACT.Exp,
+                    bias=nmax_t[u][:, jj:jj + 1], scale=1.0, accum_out=ssum_t[u][:, jj:jj + 1],
                 )
-            nc.sync.dma_start(out=out_v[a], in_=o_sb[:])
+
+        def recip(u):
+            rinv_t[u] = st.tile([P, JU], F32, name="rinv")
+            nc.vector.reciprocal(out=rinv_t[u][:], in_=ssum_t[u][:])
+
+        def norm(u):
+            mask_t[u] = mp.tile([P, JU, N], BF16, name="mask")
+            for jj in range(JU):
+                nc.gpsimd.tensor_scalar(
+                    out=mask_t[u][:, jj, :], in0=z_t[u][:, jj, :], scalar1=rinv_t[u][:, jj:jj + 1],
+                    scalar2=0.0, op0=ALU.mult, op1=ALU.add,
+                )
+
+        def transp(u):
+            pt_t[u] = []
+            for half in range(2):
+                pt = psum_t.tile([P, 2, PACK, P], BF16, name="pt")
+                pt_t[u].append(pt)
+                for q in range(2):
+                    jj = 2 * half + q
+                    for t in range(PACK):
+                        nc.tensor.transpose(pt[:, q, t, :], mask_t[u][:, jj, t * P:(t + 1) * P], ident[:])
+
+        def copy_out(u):
+            grp_t[u] = gp.tile([P, JU, P, PACK], BF16, name="grp", align_bytes=64)
+            for half in range(2):
+                nc.scalar.copy(
+                    out=grp_t[u][:, 2 * half:2 * half + 2, :, :],
+                    in_=pt_t[u][half][:].rearrange("p q t n -> p q n t"),
+                )
+
+        def quant(u):
+            codes_t[u] = cp.tile([P, JU * P], U32, name="codes", align_bytes=64)
+            scl_t[u] = cp.tile([P, JU * P], U8, name="scl", align_bytes=64)
+            nc.vector.quantize_mx(
+                out=codes_t[u][:].bitcast(FP8X4), scales=scl_t[u][:],
+                in_=grp_t[u][:].rearrange("p j n t -> p (j n t)"),
+            )
+
+        def mx(u):
+            a, j0 = UNITS[u]
+            if u % 2 == 0:
+                po_t[u // 2] = psum_o.tile([P, 2 * JU, B], F32, name="po")
+            po = po_t[u // 2]
+            for jj in range(JU):
+                j = j0 + jj
+                nc.tensor.matmul_mx(
+                    out=po[:, JU * (u % 2) + jj, :],
+                    lhsT=codes_t[u][:, jj * P:(jj + 1) * P].bitcast(FP8X4),
+                    lhsT_scale=scl_t[u][:, jj * P:(jj + 1) * P],
+                    rhs=x_codes[:, j * B:(j + 1) * B].bitcast(FP8X4),
+                    rhs_scale=x_scl[:, j * B:(j + 1) * B],
+                    start=True, stop=True,
+                )
+
+        def evac(u):
+            a, j0 = UNITS[u]
+            if u % UPA == 1:
+                o_t[a] = op.tile([P, B, J], F32, name="o_sb")
+            jb = j0 - JU
+            nc.scalar.copy(
+                out=o_t[a][:, :, jb:jb + 2 * JU], in_=po_t[u // 2][:].rearrange("p j b -> p b j"),
+            )
+            if u % UPA == UPA - 1:
+                nc.sync.dma_start(out=out_v[a], in_=o_t[a][:])
+
+        def ok(u):
+            return 0 <= u < NU
+
+        for u in range(PREFETCH):
+            load(u)
+        for k in range(NU + LAG_EV + 1):
+            if ok(k + PREFETCH):
+                load(k + PREFETCH)
+            if ok(k - LAG_E):
+                exps(k - LAG_E)
+            if ok(k - LAG_C):
+                copy_out(k - LAG_C)
+            if ok(k - LAG_EV) and (k - LAG_EV) % 2 == 1:
+                evac(k - LAG_EV)
+            if ok(k - LAG_N):
+                norm(k - LAG_N)
+            if 0 <= k - X_STEP < UPA:
+                x_group(k - X_STEP)
+            if ok(k):
+                add_max(k)
+            if ok(k - LAG_Q):
+                quant(k - LAG_Q)
+            if 0 <= k - X_STEP - 1 < UPA:
+                x_quant(k - X_STEP - 1)
+            if ok(k - LAG_R):
+                recip(k - LAG_R)
+            if ok(k - LAG_T):
+                transp(k - LAG_T)
+            if ok(k - LAG_MX):
+                mx(k - LAG_MX)

@@ -23,16 +23,25 @@ UNITS = [(a, j0) for a in range(NT) for j0 in range(0, J, JU)]
 NU = len(UNITS)
 UPA = J // JU
 
-LAG_E = 1
-LAG_R = 1
-LAG_N = 2
-LAG_T = 2
-LAG_C = 3
-LAG_Q = 4
-LAG_MX = 10
-LAG_EV = 11
+PREFETCH = 6
 X_STEP = 7
-PREFETCH = 3
+N_ON_V_FROM = 30
+C_SPLIT_FROM = 29
+
+
+def norm_on_vector(u, jj):
+    return u >= N_ON_V_FROM
+
+
+def step_tables():
+    s_n, s_c, s_q, s_mx = {}, {}, {}, {}
+    for u in range(NU):
+        s_n[u] = u + 1 if u >= N_ON_V_FROM else u + 2
+        s_c[u] = s_n[u] + 1
+        s_q[u] = s_c[u] + 1
+        early = X_STEP + 3 + u if u < UPA else X_STEP + 3 + UPA + (u - UPA) // 2
+        s_mx[u] = max(s_q[u] + 1, early)
+    return s_n, s_c, s_q, s_mx
 
 
 def tile_learnablemasktemporalaggregation_kernel(tc, x, learnable_offset, predefined_weights, out):
@@ -41,6 +50,7 @@ def tile_learnablemasktemporalaggregation_kernel(tc, x, learnable_offset, predef
     pre_v = predefined_weights.rearrange("(a p) m -> p a m", p=P)
     x_v = x.rearrange("b (t p) j -> p (b t) j", p=P)
     out_v = out.rearrange("b (a p) j -> a p b j", p=P)
+    s_n, s_c, s_q, s_mx = step_tables()
 
     with ExitStack() as ctx:
         const = ctx.enter_context(tc.tile_pool(name="const", bufs=1))
@@ -49,7 +59,7 @@ def tile_learnablemasktemporalaggregation_kernel(tc, x, learnable_offset, predef
         st = ctx.enter_context(tc.tile_pool(name="st", bufs=6))
         mp = ctx.enter_context(tc.tile_pool(name="mp", bufs=3))
         gp = ctx.enter_context(tc.tile_pool(name="gp", bufs=3))
-        cp = ctx.enter_context(tc.tile_pool(name="cp", bufs=LAG_MX - LAG_Q + 2))
+        cp = ctx.enter_context(tc.tile_pool(name="cp", bufs=9))
         op = ctx.enter_context(tc.tile_pool(name="op", bufs=2))
         psum_c = ctx.enter_context(tc.psum_pool(name="psum_c", bufs=1))
         psum_t = ctx.enter_context(tc.psum_pool(name="psum_t", bufs=4))
@@ -59,20 +69,21 @@ def tile_learnablemasktemporalaggregation_kernel(tc, x, learnable_offset, predef
         off_t, z_t, nmax_t, ssum_t, rinv_t, mask_t = {}, {}, {}, {}, {}, {}
         pt_t, grp_t, codes_t, scl_t, po_t, o_t = {}, {}, {}, {}, {}, {}
 
-        pre_sb = const.tile([P, NT, N], BF16)
-        nc.sync.dma_start(out=pre_sb[:], in_=pre_v)
-        x_raw = const.tile([P, B * PACK, J], BF16)
-        for c in range(4):
-            nc.gpsimd.dma_start(out=x_raw[:, 64 * c:64 * (c + 1), :], in_=x_v[:, 64 * c:64 * (c + 1), :])
         ident = const.tile([P, P], BF16)
         make_identity(nc, ident[:])
+        pre_sb = const.tile([P, NT, N], BF16)
+        nc.sync.dma_start(out=pre_sb[:], in_=pre_v)
         pre_ps = [psum_c.tile([P, 2, N], BF16, name="pre_ps%d" % i) for i in range(2)]
         for a in range(NT):
             nc.tensor.matmul(out=pre_ps[a // 2][:, a % 2, :], lhsT=ident[:], rhs=pre_sb[:, a, :], start=True, stop=True)
 
+        x_raw = const.tile([P, B * PACK, J], BF16)
         x_grp = const.tile([P, J, B * PACK], BF16, align_bytes=64)
         x_codes = const.tile([P, J * B], U32, align_bytes=64)
         x_scl = const.tile([P, J * B], U8, align_bytes=64)
+
+        def x_load(c):
+            nc.sync.dma_start(out=x_raw[:, 32 * c:32 * (c + 1), :], in_=x_v[:, 32 * c:32 * (c + 1), :])
 
         def x_group(c):
             nc.gpsimd.tensor_scalar(
@@ -116,13 +127,22 @@ def tile_learnablemasktemporalaggregation_kernel(tc, x, learnable_offset, predef
             rinv_t[u] = st.tile([P, JU], F32, name="rinv")
             nc.vector.reciprocal(out=rinv_t[u][:], in_=ssum_t[u][:])
 
-        def norm(u):
-            mask_t[u] = mp.tile([P, JU, N], BF16, name="mask")
+        def norm(u, on_vector):
+            if u not in mask_t:
+                mask_t[u] = mp.tile([P, JU, N], BF16, name="mask")
             for jj in range(JU):
-                nc.gpsimd.tensor_scalar(
-                    out=mask_t[u][:, jj, :], in0=z_t[u][:, jj, :], scalar1=rinv_t[u][:, jj:jj + 1],
-                    scalar2=0.0, op0=ALU.mult, op1=ALU.add,
-                )
+                if norm_on_vector(u, jj) != on_vector:
+                    continue
+                if on_vector:
+                    nc.vector.tensor_scalar(
+                        out=mask_t[u][:, jj, :], in0=z_t[u][:, jj, :], scalar1=rinv_t[u][:, jj:jj + 1],
+                        scalar2=None, op0=ALU.mult,
+                    )
+                else:
+                    nc.gpsimd.tensor_scalar(
+                        out=mask_t[u][:, jj, :], in0=z_t[u][:, jj, :], scalar1=rinv_t[u][:, jj:jj + 1],
+                        scalar2=0.0, op0=ALU.mult, op1=ALU.add,
+                    )
 
         def transp(u):
             pt_t[u] = []
@@ -134,13 +154,15 @@ def tile_learnablemasktemporalaggregation_kernel(tc, x, learnable_offset, predef
                     for t in range(PACK):
                         nc.tensor.transpose(pt[:, q, t, :], mask_t[u][:, jj, t * P:(t + 1) * P], ident[:])
 
-        def copy_out(u):
-            grp_t[u] = gp.tile([P, JU, P, PACK], BF16, name="grp", align_bytes=64)
-            for half in range(2):
-                nc.scalar.copy(
-                    out=grp_t[u][:, 2 * half:2 * half + 2, :, :],
-                    in_=pt_t[u][half][:].rearrange("p q t n -> p q n t"),
-                )
+        def copy_out(u, half, on_vector):
+            if u not in grp_t:
+                grp_t[u] = gp.tile([P, JU, P, PACK], BF16, name="grp", align_bytes=64)
+            dst = grp_t[u][:, 2 * half:2 * half + 2, :, :]
+            src = pt_t[u][half][:].rearrange("p q t n -> p q n t")
+            if on_vector:
+                nc.vector.tensor_copy(out=dst, in_=src)
+            else:
+                nc.scalar.copy(out=dst, in_=src)
 
         def quant(u):
             codes_t[u] = cp.tile([P, JU * P], U32, name="codes", align_bytes=64)
@@ -177,33 +199,48 @@ def tile_learnablemasktemporalaggregation_kernel(tc, x, learnable_offset, predef
             if u % UPA == UPA - 1:
                 nc.sync.dma_start(out=out_v[a], in_=o_t[a][:])
 
-        def ok(u):
-            return 0 <= u < NU
+        def at(table, k):
+            return [u for u in range(NU) if table[u] == k]
 
+        xl = 0
         for u in range(PREFETCH):
             load(u)
-        for k in range(NU + LAG_EV + 1):
-            if ok(k + PREFETCH):
+            if u >= 1:
+                x_load(xl)
+                xl += 1
+        for k in range(max(s_mx[u] for u in range(NU)) + 2):
+            if k + PREFETCH < NU:
                 load(k + PREFETCH)
-            if ok(k - LAG_E):
-                exps(k - LAG_E)
-            if ok(k - LAG_C):
-                copy_out(k - LAG_C)
-            if ok(k - LAG_EV) and (k - LAG_EV) % 2 == 1:
-                evac(k - LAG_EV)
-            if ok(k - LAG_N):
-                norm(k - LAG_N)
+            if xl < 8:
+                x_load(xl)
+                xl += 1
+            if 0 <= k - 1 < NU:
+                exps(k - 1)
+            for u in at(s_c, k):
+                copy_out(u, 0, False)
+                if u < C_SPLIT_FROM:
+                    copy_out(u, 1, False)
+            for u in at(s_mx, k - 1):
+                if u % 2 == 1:
+                    evac(u)
+            for u in at(s_n, k):
+                norm(u, False)
             if 0 <= k - X_STEP < UPA:
                 x_group(k - X_STEP)
-            if ok(k):
+            if k < NU:
                 add_max(k)
-            if ok(k - LAG_Q):
-                quant(k - LAG_Q)
+            for u in at(s_c, k):
+                if u >= C_SPLIT_FROM:
+                    copy_out(u, 1, True)
+            for u in at(s_q, k):
+                quant(u)
             if 0 <= k - X_STEP - 1 < UPA:
                 x_quant(k - X_STEP - 1)
-            if ok(k - LAG_R):
-                recip(k - LAG_R)
-            if ok(k - LAG_T):
-                transp(k - LAG_T)
-            if ok(k - LAG_MX):
-                mx(k - LAG_MX)
+            if 0 <= k - 1 < NU:
+                recip(k - 1)
+            for u in at(s_n, k):
+                norm(u, True)
+            for u in at(s_n, k):
+                transp(u)
+            for u in at(s_mx, k):
+                mx(u)

@@ -18,28 +18,38 @@ P = 128
 B, N, J = 64, 512, 32
 NT = N // P
 PACK = 4
-JU = 4
-UNITS = [(a, j0) for a in range(NT) for j0 in range(0, J, JU)]
-NU = len(UNITS)
-UPA = J // JU
-
+BANK_J = 8
+SIZES = [4] * 29 + [2] * 4 + [1] * 4
 PREFETCH = 6
 X_STEP = 7
-N_ON_V_FROM = 30
-C_SPLIT_FROM = 29
+TAIL_N = 2
+TAIL_C = 4
+XJ = 4
 
 
-def norm_on_vector(u, jj):
-    return u >= N_ON_V_FROM
+def make_units():
+    units = []
+    j = 0
+    for nj in SIZES:
+        units.append((j // J, j % J, nj))
+        j += nj
+    assert j == NT * J
+    return units
+
+
+UNITS = make_units()
+NU = len(UNITS)
 
 
 def step_tables():
     s_n, s_c, s_q, s_mx = {}, {}, {}, {}
     for u in range(NU):
-        s_n[u] = u + 1 if u >= N_ON_V_FROM else u + 2
+        s_n[u] = u + 1 if u >= NU - TAIL_N else u + 2
+        if u > 0:
+            s_n[u] = max(s_n[u], s_n[u - 1])
         s_c[u] = s_n[u] + 1
         s_q[u] = s_c[u] + 1
-        early = X_STEP + 3 + u if u < UPA else X_STEP + 3 + UPA + (u - UPA) // 2
+        early = X_STEP + 3 + u if u < 8 else X_STEP + 11 + (u - 8) // 2
         s_mx[u] = max(s_q[u] + 1, early)
     return s_n, s_c, s_q, s_mx
 
@@ -55,8 +65,8 @@ def tile_learnablemasktemporalaggregation_kernel(tc, x, learnable_offset, predef
     with ExitStack() as ctx:
         const = ctx.enter_context(tc.tile_pool(name="const", bufs=1))
         ld = ctx.enter_context(tc.tile_pool(name="ld", bufs=PREFETCH + 1))
-        zp = ctx.enter_context(tc.tile_pool(name="zp", bufs=4))
-        st = ctx.enter_context(tc.tile_pool(name="st", bufs=6))
+        zp = ctx.enter_context(tc.tile_pool(name="zp", bufs=5))
+        st = ctx.enter_context(tc.tile_pool(name="st", bufs=8))
         mp = ctx.enter_context(tc.tile_pool(name="mp", bufs=3))
         gp = ctx.enter_context(tc.tile_pool(name="gp", bufs=3))
         cp = ctx.enter_context(tc.tile_pool(name="cp", bufs=9))
@@ -87,53 +97,64 @@ def tile_learnablemasktemporalaggregation_kernel(tc, x, learnable_offset, predef
 
         def x_group(c):
             nc.gpsimd.tensor_scalar(
-                out=x_grp[:, JU * c:JU * (c + 1), :],
-                in0=x_raw[:, :, JU * c:JU * (c + 1)].rearrange("p c j -> p j c"),
+                out=x_grp[:, XJ * c:XJ * (c + 1), :],
+                in0=x_raw[:, :, XJ * c:XJ * (c + 1)].rearrange("p c j -> p j c"),
                 scalar1=1.0, scalar2=0.0, op0=ALU.mult, op1=ALU.add,
             )
 
         def x_quant(c):
-            w = JU * B
+            w = XJ * B
             nc.vector.quantize_mx(
                 out=x_codes[:, w * c:w * (c + 1)].bitcast(FP8X4),
                 scales=x_scl[:, w * c:w * (c + 1)],
-                in_=x_grp[:, JU * c:JU * (c + 1), :].rearrange("p j c -> p (j c)"),
+                in_=x_grp[:, XJ * c:XJ * (c + 1), :].rearrange("p j c -> p (j c)"),
             )
 
         def load(u):
-            a, j0 = UNITS[u]
-            off_t[u] = ld.tile([P, JU, N], BF16, name="off")
-            nc.sync.dma_start(out=off_t[u][:], in_=off_v[a][:, j0:j0 + JU, :])
+            a, j0, nj = UNITS[u]
+            off_t[u] = ld.tile([P, nj, N], BF16, name="off")
+            nc.sync.dma_start(out=off_t[u][:], in_=off_v[a][:, j0:j0 + nj, :])
+
+        def g_share(u):
+            return 1 if (UNITS[u][2] == 4 and u % 2 == 1) else 0
+
+        def add_gpsimd(u):
+            a, j0, nj = UNITS[u]
+            z_t[u] = zp.tile([P, nj, N], F32, name="z")
+            for jj in range(nj - g_share(u), nj):
+                nc.gpsimd.tensor_tensor(
+                    out=z_t[u][:, jj, :], in0=off_t[u][:, jj, :], in1=pre_sb[:, a, :], op=ALU.add,
+                )
 
         def add_max(u):
-            a, j0 = UNITS[u]
-            z_t[u] = zp.tile([P, JU, N], F32, name="z")
+            a, j0, nj = UNITS[u]
+            nv = nj - g_share(u)
             nc.vector.tensor_tensor(
-                out=z_t[u][:], in0=off_t[u][:],
-                in1=pre_ps[a // 2][:, a % 2:a % 2 + 1, :].to_broadcast([P, JU, N]), op=ALU.add,
+                out=z_t[u][:, 0:nv, :], in0=off_t[u][:, 0:nv, :],
+                in1=pre_ps[a // 2][:, a % 2:a % 2 + 1, :].to_broadcast([P, nv, N]), op=ALU.add,
             )
-            nmax_t[u] = st.tile([P, JU], F32, name="nmax")
+            nmax_t[u] = st.tile([P, nj], F32, name="nmax")
             nc.vector.tensor_reduce(out=nmax_t[u][:], in_=z_t[u][:], axis=AX.X, op=ALU.max, negate=True)
 
         def exps(u):
-            ssum_t[u] = st.tile([P, JU], F32, name="ssum")
-            for jj in range(JU):
+            a, j0, nj = UNITS[u]
+            ssum_t[u] = st.tile([P, nj], F32, name="ssum")
+            for jj in range(nj):
                 nc.scalar.activation(
                     out=z_t[u][:, jj, :], in_=z_t[u][:, jj, :], func=ACT.Exp,
                     bias=nmax_t[u][:, jj:jj + 1], scale=1.0, accum_out=ssum_t[u][:, jj:jj + 1],
                 )
 
         def recip(u):
-            rinv_t[u] = st.tile([P, JU], F32, name="rinv")
+            a, j0, nj = UNITS[u]
+            rinv_t[u] = st.tile([P, nj], F32, name="rinv")
             nc.vector.reciprocal(out=rinv_t[u][:], in_=ssum_t[u][:])
 
-        def norm(u, on_vector):
-            if u not in mask_t:
-                mask_t[u] = mp.tile([P, JU, N], BF16, name="mask")
-            for jj in range(JU):
-                if norm_on_vector(u, jj) != on_vector:
-                    continue
-                if on_vector:
+        def norm(u):
+            a, j0, nj = UNITS[u]
+            mask_t[u] = mp.tile([P, nj, N], BF16, name="mask")
+            for jj in range(nj):
+                if u >= NU - TAIL_N:
                     nc.vector.tensor_scalar(
                         out=mask_t[u][:, jj, :], in0=z_t[u][:, jj, :], scalar1=rinv_t[u][:, jj:jj + 1],
                         scalar2=None, op0=ALU.mult,
@@ -144,43 +165,54 @@ def tile_learnablemasktemporalaggregation_kernel(tc, x, learnable_offset, predef
                         scalar2=0.0, op0=ALU.mult, op1=ALU.add,
                     )
 
+        def pieces(u):
+            nj = UNITS[u][2]
+            return [(q0, min(2, nj - q0)) for q0 in range(0, nj, 2)]
+
         def transp(u):
             pt_t[u] = []
-            for half in range(2):
-                pt = psum_t.tile([P, 2, PACK, P], BF16, name="pt")
+            for q0, nq in pieces(u):
+                pt = psum_t.tile([P, nq, PACK, P], BF16, name="pt")
                 pt_t[u].append(pt)
-                for q in range(2):
-                    jj = 2 * half + q
+                for q in range(nq):
                     for t in range(PACK):
-                        nc.tensor.transpose(pt[:, q, t, :], mask_t[u][:, jj, t * P:(t + 1) * P], ident[:])
+                        nc.tensor.transpose(pt[:, q, t, :], mask_t[u][:, q0 + q, t * P:(t + 1) * P], ident[:])
 
-        def copy_out(u, half, on_vector):
+        def copy_on_vector(u, i):
+            return u >= NU - TAIL_C and (u + i) % 2 == 1
+
+        def copy_out(u, on_vector):
+            a, j0, nj = UNITS[u]
             if u not in grp_t:
-                grp_t[u] = gp.tile([P, JU, P, PACK], BF16, name="grp", align_bytes=64)
-            dst = grp_t[u][:, 2 * half:2 * half + 2, :, :]
-            src = pt_t[u][half][:].rearrange("p q t n -> p q n t")
-            if on_vector:
-                nc.vector.tensor_copy(out=dst, in_=src)
-            else:
-                nc.scalar.copy(out=dst, in_=src)
+                grp_t[u] = gp.tile([P, nj, P, PACK], BF16, name="grp", align_bytes=64)
+            for i, (q0, nq) in enumerate(pieces(u)):
+                if copy_on_vector(u, i) != on_vector:
+                    continue
+                dst = grp_t[u][:, q0:q0 + nq, :, :]
+                src = pt_t[u][i][:].rearrange("p q t n -> p q n t")
+                if on_vector:
+                    nc.vector.tensor_copy(out=dst, in_=src)
+                else:
+                    nc.scalar.copy(out=dst, in_=src)
 
         def quant(u):
-            codes_t[u] = cp.tile([P, JU * P], U32, name="codes", align_bytes=64)
-            scl_t[u] = cp.tile([P, JU * P], U8, name="scl", align_bytes=64)
+            a, j0, nj = UNITS[u]
+            codes_t[u] = cp.tile([P, nj * P], U32, name="codes", align_bytes=64)
+            scl_t[u] = cp.tile([P, nj * P], U8, name="scl", align_bytes=64)
             nc.vector.quantize_mx(
                 out=codes_t[u][:].bitcast(FP8X4), scales=scl_t[u][:],
                 in_=grp_t[u][:].rearrange("p j n t -> p (j n t)"),
             )
 
         def mx(u):
-            a, j0 = UNITS[u]
-            if u % 2 == 0:
-                po_t[u // 2] = psum_o.tile([P, 2 * JU, B], F32, name="po")
-            po = po_t[u // 2]
-            for jj in range(JU):
+            a, j0, nj = UNITS[u]
+            bank = (a, j0 // BANK_J)
+            if j0 % BANK_J == 0:
+                po_t[bank] = psum_o.tile([P, BANK_J, B], F32, name="po")
+            for jj in range(nj):
                 j = j0 + jj
                 nc.tensor.matmul_mx(
-                    out=po[:, JU * (u % 2) + jj, :],
+                    out=po_t[bank][:, j % BANK_J, :],
                     lhsT=codes_t[u][:, jj * P:(jj + 1) * P].bitcast(FP8X4),
                     lhsT_scale=scl_t[u][:, jj * P:(jj + 1) * P],
                     rhs=x_codes[:, j * B:(j + 1) * B].bitcast(FP8X4),
@@ -189,14 +221,16 @@ def tile_learnablemasktemporalaggregation_kernel(tc, x, learnable_offset, predef
                 )
 
         def evac(u):
-            a, j0 = UNITS[u]
-            if u % UPA == 1:
+            a, j0, nj = UNITS[u]
+            if (j0 + nj) % BANK_J != 0:
+                return
+            jb = j0 + nj - BANK_J
+            if jb == 0:
                 o_t[a] = op.tile([P, B, J], F32, name="o_sb")
-            jb = j0 - JU
             nc.scalar.copy(
-                out=o_t[a][:, :, jb:jb + 2 * JU], in_=po_t[u // 2][:].rearrange("p j b -> p b j"),
+                out=o_t[a][:, :, jb:jb + BANK_J], in_=po_t[(a, jb // BANK_J)][:].rearrange("p j b -> p b j"),
             )
-            if u % UPA == UPA - 1:
+            if jb + BANK_J == J:
                 nc.sync.dma_start(out=out_v[a], in_=o_t[a][:])
 
         def at(table, k):
@@ -208,6 +242,7 @@ def tile_learnablemasktemporalaggregation_kernel(tc, x, learnable_offset, predef
             if u >= 1:
                 x_load(xl)
                 xl += 1
+        add_gpsimd(0)
         for k in range(max(s_mx[u] for u in range(NU)) + 2):
             if k + PREFETCH < NU:
                 load(k + PREFETCH)
@@ -217,29 +252,29 @@ def tile_learnablemasktemporalaggregation_kernel(tc, x, learnable_offset, predef
             if 0 <= k - 1 < NU:
                 exps(k - 1)
             for u in at(s_c, k):
-                copy_out(u, 0, False)
-                if u < C_SPLIT_FROM:
-                    copy_out(u, 1, False)
+                copy_out(u, False)
             for u in at(s_mx, k - 1):
-                if u % 2 == 1:
-                    evac(u)
+                evac(u)
             for u in at(s_n, k):
-                norm(u, False)
-            if 0 <= k - X_STEP < UPA:
+                if u < NU - TAIL_N:
+                    norm(u)
+            if k + 1 < NU:
+                add_gpsimd(k + 1)
+            if 0 <= k - X_STEP < 8:
                 x_group(k - X_STEP)
             if k < NU:
                 add_max(k)
             for u in at(s_c, k):
-                if u >= C_SPLIT_FROM:
-                    copy_out(u, 1, True)
+                copy_out(u, True)
             for u in at(s_q, k):
                 quant(u)
-            if 0 <= k - X_STEP - 1 < UPA:
+            if 0 <= k - X_STEP - 1 < 8:
                 x_quant(k - X_STEP - 1)
             if 0 <= k - 1 < NU:
                 recip(k - 1)
             for u in at(s_n, k):
-                norm(u, True)
+                if u >= NU - TAIL_N:
+                    norm(u)
             for u in at(s_n, k):
                 transp(u)
             for u in at(s_mx, k):

@@ -116,7 +116,7 @@ def tile_learnablemasktemporalaggregation_kernel(tc, x, learnable_offset, predef
             nc.sync.dma_start(out=off_t[u][:], in_=off_v[a][:, j0:j0 + nj, :])
 
         def g_share(u):
-            return 1 if (UNITS[u][2] == 4 and u % 2 == 1) else 0
+            return 0
 
         def add_gpsimd(u):
             a, j0, nj = UNITS[u]

@@ -19,12 +19,15 @@ B, N, J = 64, 512, 32
 NT = N // P
 PACK = 4
 BANK_J = 8
-SIZES = [4] * 29 + [2] * 4 + [1] * 4
-PREFETCH = 6
-X_STEP = 7
+SIZES = [1, 1, 2] + [4] * 31
+PREFETCH = 8
+X_STEP = 9
 TAIL_N = 2
-TAIL_C = 4
+TAIL_C = 3
 XJ = 4
+AHEAD = 1
+SBUF_PRE_UNITS = 2
+X_AFTER = 3
 
 
 def make_units():
@@ -49,8 +52,14 @@ def step_tables():
             s_n[u] = max(s_n[u], s_n[u - 1])
         s_c[u] = s_n[u] + 1
         s_q[u] = s_c[u] + 1
-        early = X_STEP + 3 + u if u < 8 else X_STEP + 11 + (u - 8) // 2
-        s_mx[u] = max(s_q[u] + 1, early)
+        a, j0, nj = UNITS[u]
+        s_mx[u] = s_q[u] + 1
+        if a == 0:
+            s_mx[u] = max(s_mx[u], X_STEP + 2 + (j0 + nj - 1) // XJ)
+        if u > 0:
+            s_mx[u] = max(s_mx[u], s_mx[u - 1])
+        if u > 1:
+            s_mx[u] = max(s_mx[u], s_mx[u - 2] + 1)
     return s_n, s_c, s_q, s_mx
 
 
@@ -82,10 +91,8 @@ def tile_learnablemasktemporalaggregation_kernel(tc, x, learnable_offset, predef
         ident = const.tile([P, P], BF16)
         make_identity(nc, ident[:])
         pre_sb = const.tile([P, NT, N], BF16)
-        nc.sync.dma_start(out=pre_sb[:], in_=pre_v)
+        nc.sync.dma_start(out=pre_sb[:, 0:1, :], in_=pre_v[:, 0:1, :])
         pre_ps = [psum_c.tile([P, 2, N], BF16, name="pre_ps%d" % i) for i in range(2)]
-        for a in range(NT):
-            nc.tensor.matmul(out=pre_ps[a // 2][:, a % 2, :], lhsT=ident[:], rhs=pre_sb[:, a, :], start=True, stop=True)
 
         x_raw = const.tile([P, B * PACK, J], BF16)
         x_grp = const.tile([P, J, B * PACK], BF16, align_bytes=64)
@@ -115,24 +122,19 @@ def tile_learnablemasktemporalaggregation_kernel(tc, x, learnable_offset, predef
             off_t[u] = ld.tile([P, nj, N], BF16, name="off")
             nc.sync.dma_start(out=off_t[u][:], in_=off_v[a][:, j0:j0 + nj, :])
 
-        def g_share(u):
-            return 0
-
-        def add_gpsimd(u):
+        def add(u):
             a, j0, nj = UNITS[u]
             z_t[u] = zp.tile([P, nj, N], F32, name="z")
-            for jj in range(nj - g_share(u), nj):
-                nc.gpsimd.tensor_tensor(
-                    out=z_t[u][:, jj, :], in0=off_t[u][:, jj, :], in1=pre_sb[:, a, :], op=ALU.add,
-                )
-
-        def add_max(u):
-            a, j0, nj = UNITS[u]
-            nv = nj - g_share(u)
+            if u < SBUF_PRE_UNITS:
+                pre_ap = pre_sb[:, a:a + 1, :]
+            else:
+                pre_ap = pre_ps[a // 2][:, a % 2:a % 2 + 1, :]
             nc.vector.tensor_tensor(
-                out=z_t[u][:, 0:nv, :], in0=off_t[u][:, 0:nv, :],
-                in1=pre_ps[a // 2][:, a % 2:a % 2 + 1, :].to_broadcast([P, nv, N]), op=ALU.add,
+                out=z_t[u][:], in0=off_t[u][:], in1=pre_ap.to_broadcast([P, nj, N]), op=ALU.add,
             )
+
+        def rowmax(u):
+            a, j0, nj = UNITS[u]
             nmax_t[u] = st.tile([P, nj], F32, name="nmax")
             nc.vector.tensor_reduce(out=nmax_t[u][:], in_=z_t[u][:], axis=AX.X, op=ALU.max, negate=True)
 
@@ -239,10 +241,15 @@ def tile_learnablemasktemporalaggregation_kernel(tc, x, learnable_offset, predef
         xl = 0
         for u in range(PREFETCH):
             load(u)
-            if u >= 1:
+            if u == 0:
+                nc.sync.dma_start(out=pre_sb[:, 1:NT, :], in_=pre_v[:, 1:NT, :])
+            if u >= X_AFTER:
                 x_load(xl)
                 xl += 1
-        add_gpsimd(0)
+        for a in range(NT):
+            nc.tensor.matmul(out=pre_ps[a // 2][:, a % 2, :], lhsT=ident[:], rhs=pre_sb[:, a, :], start=True, stop=True)
+        for u in range(AHEAD):
+            add(u)
         for k in range(max(s_mx[u] for u in range(NU)) + 2):
             if k + PREFETCH < NU:
                 load(k + PREFETCH)
@@ -258,12 +265,12 @@ def tile_learnablemasktemporalaggregation_kernel(tc, x, learnable_offset, predef
             for u in at(s_n, k):
                 if u < NU - TAIL_N:
                     norm(u)
-            if k + 1 < NU:
-                add_gpsimd(k + 1)
             if 0 <= k - X_STEP < 8:
                 x_group(k - X_STEP)
+            if k + AHEAD < NU:
+                add(k + AHEAD)
             if k < NU:
-                add_max(k)
+                rowmax(k)
             for u in at(s_c, k):
                 copy_out(u, True)
             for u in at(s_q, k):

@@ -20,8 +20,8 @@ NT = N // P
 PACK = 4
 BANK_J = 8
 SIZES = [1, 1, 2] + [4] * 31
-PREFETCH = 8
-X_STEP = 9
+PREFETCH = 6
+X_STEP = 8
 TAIL_N = 2
 TAIL_C = 3
 XJ = 4
@@ -67,7 +67,7 @@ def tile_learnablemasktemporalaggregation_kernel(tc, x, learnable_offset, predef
     nc = tc.nc
     off_v = learnable_offset.rearrange("j (a p) m -> a p j m", p=P)
     pre_v = predefined_weights.rearrange("(a p) m -> p a m", p=P)
-    x_v = x.rearrange("b (t p) j -> p (b t) j", p=P)
+    x_v = x.rearrange("b (p t) j -> p b (t j)", t=PACK)
     out_v = out.rearrange("b (a p) j -> a p b j", p=P)
     s_n, s_c, s_q, s_mx = step_tables()
 
@@ -94,18 +94,19 @@ def tile_learnablemasktemporalaggregation_kernel(tc, x, learnable_offset, predef
         nc.sync.dma_start(out=pre_sb[:, 0:1, :], in_=pre_v[:, 0:1, :])
         pre_ps = [psum_c.tile([P, 2, N], BF16, name="pre_ps%d" % i) for i in range(2)]
 
-        x_raw = const.tile([P, B * PACK, J], BF16)
+        x_raw = const.tile([P, B, PACK * J], BF16)
+        x_raw_v = x_raw[:].rearrange("p b (t j) -> p (b t) j", j=J)
         x_grp = const.tile([P, J, B * PACK], BF16, align_bytes=64)
         x_codes = const.tile([P, J * B], U32, align_bytes=64)
         x_scl = const.tile([P, J * B], U8, align_bytes=64)
 
         def x_load(c):
-            nc.sync.dma_start(out=x_raw[:, 32 * c:32 * (c + 1), :], in_=x_v[:, 32 * c:32 * (c + 1), :])
+            nc.sync.dma_start(out=x_raw[:, 8 * c:8 * (c + 1), :], in_=x_v[:, 8 * c:8 * (c + 1), :])
 
         def x_group(c):
             nc.gpsimd.tensor_scalar(
                 out=x_grp[:, XJ * c:XJ * (c + 1), :],
-                in0=x_raw[:, :, XJ * c:XJ * (c + 1)].rearrange("p c j -> p j c"),
+                in0=x_raw_v[:, :, XJ * c:XJ * (c + 1)].rearrange("p c j -> p j c"),
                 scalar1=1.0, scalar2=0.0, op0=ALU.mult, op1=ALU.add,
             )
 
@@ -130,7 +131,10 @@ def tile_learnablemasktemporalaggregation_kernel(tc, x, learnable_offset, predef
             else:
                 pre_ap = pre_ps[a // 2][:, a % 2:a % 2 + 1, :]
             nc.vector.tensor_tensor(
-                out=z_t[u][:], in0=off_t[u][:], in1=pre_ap.to_broadcast([P, nj, N]), op=ALU.add,
+                out=z_t[u][:].rearrange("p j (t c) -> p j t c", t=PACK),
+                in0=off_t[u][:].rearrange("p j (c t) -> p j t c", t=PACK),
+                in1=pre_ap.rearrange("p o (c t) -> p o t c", t=PACK).to_broadcast([P, nj, PACK, P]),
+                op=ALU.add,
             )
 
         def rowmax(u):

@@ -19,15 +19,15 @@ B, N, J = 64, 512, 32
 NT = N // P
 PACK = 4
 BANK_J = 8
-SIZES = [1, 1, 2] + [4] * 31
+SIZES = [4] * 32
 PREFETCH = 6
-X_STEP = 8
+X_STEP = 7
 TAIL_N = 2
 TAIL_C = 3
 XJ = 4
 AHEAD = 1
-SBUF_PRE_UNITS = 2
-X_AFTER = 3
+SBUF_PRE_UNITS = 0
+X_AFTER = 1
 
 
 def make_units():
@@ -67,7 +67,7 @@ def tile_learnablemasktemporalaggregation_kernel(tc, x, learnable_offset, predef
     nc = tc.nc
     off_v = learnable_offset.rearrange("j (a p) m -> a p j m", p=P)
     pre_v = predefined_weights.rearrange("(a p) m -> p a m", p=P)
-    x_v = x.rearrange("b (p t) j -> p b (t j)", t=PACK)
+    x_v = x.rearrange("b (t p) j -> p (b t) j", p=P)
     out_v = out.rearrange("b (a p) j -> a p b j", p=P)
     s_n, s_c, s_q, s_mx = step_tables()
 
@@ -94,19 +94,18 @@ def tile_learnablemasktemporalaggregation_kernel(tc, x, learnable_offset, predef
         nc.sync.dma_start(out=pre_sb[:, 0:1, :], in_=pre_v[:, 0:1, :])
         pre_ps = [psum_c.tile([P, 2, N], BF16, name="pre_ps%d" % i) for i in range(2)]
 
-        x_raw = const.tile([P, B, PACK * J], BF16)
-        x_raw_v = x_raw[:].rearrange("p b (t j) -> p (b t) j", j=J)
+        x_raw = const.tile([P, B * PACK, J], BF16)
         x_grp = const.tile([P, J, B * PACK], BF16, align_bytes=64)
         x_codes = const.tile([P, J * B], U32, align_bytes=64)
         x_scl = const.tile([P, J * B], U8, align_bytes=64)
 
         def x_load(c):
-            nc.sync.dma_start(out=x_raw[:, 8 * c:8 * (c + 1), :], in_=x_v[:, 8 * c:8 * (c + 1), :])
+            nc.sync.dma_start(out=x_raw[:, 32 * c:32 * (c + 1), :], in_=x_v[:, 32 * c:32 * (c + 1), :])
 
         def x_group(c):
             nc.gpsimd.tensor_scalar(
                 out=x_grp[:, XJ * c:XJ * (c + 1), :],
-                in0=x_raw_v[:, :, XJ * c:XJ * (c + 1)].rearrange("p c j -> p j c"),
+                in0=x_raw[:, :, XJ * c:XJ * (c + 1)].rearrange("p c j -> p j c"),
                 scalar1=1.0, scalar2=0.0, op0=ALU.mult, op1=ALU.add,
             )
 
@@ -131,10 +130,7 @@ def tile_learnablemasktemporalaggregation_kernel(tc, x, learnable_offset, predef
             else:
                 pre_ap = pre_ps[a // 2][:, a % 2:a % 2 + 1, :]
             nc.vector.tensor_tensor(
-                out=z_t[u][:].rearrange("p j (t c) -> p j t c", t=PACK),
-                in0=off_t[u][:].rearrange("p j (c t) -> p j t c", t=PACK),
-                in1=pre_ap.rearrange("p o (c t) -> p o t c", t=PACK).to_broadcast([P, nj, PACK, P]),
-                op=ALU.add,
+                out=z_t[u][:], in0=off_t[u][:], in1=pre_ap.to_broadcast([P, nj, N]), op=ALU.add,
             )
 
         def rowmax(u):
@@ -277,12 +273,12 @@ def tile_learnablemasktemporalaggregation_kernel(tc, x, learnable_offset, predef
                 rowmax(k)
             for u in at(s_c, k):
                 copy_out(u, True)
+            if 0 <= k - 1 < NU:
+                recip(k - 1)
             for u in at(s_q, k):
                 quant(u)
             if 0 <= k - X_STEP - 1 < 8:
                 x_quant(k - X_STEP - 1)
-            if 0 <= k - 1 < NU:
-                recip(k - 1)
             for u in at(s_n, k):
                 if u >= NU - TAIL_N:
                     norm(u)

from contextlib import ExitStack

import concourse.mybir as mybir
from concourse.masks import make_identity

FLOPS = 2 * 64 * 512 * 512 * 32

BF16 = mybir.dt.bfloat16
F32 = mybir.dt.float32
U32 = mybir.dt.uint32
U8 = mybir.dt.uint8
FP8X4 = mybir.dt.float8_e4m3fn_x4
ALU = mybir.AluOpType
ACT = mybir.ActivationFunctionType
AX = mybir.AxisListType

P = 128
B, N, J = 64, 512, 32
NT = N // P
PACK = 4
BANK_J = 8
SIZES = [4] * 32
PREFETCH = 6
X_STEP = 7
TAIL_N = 2
TAIL_C = 3
XJ = 4
AHEAD = 1
SBUF_PRE_UNITS = 0
X_AFTER = 1


def make_units():
    units = []
    j = 0
    for nj in SIZES:
        units.append((j // J, j % J, nj))
        j += nj
    assert j == NT * J
    return units


UNITS = make_units()
NU = len(UNITS)


def step_tables():
    s_n, s_c, s_q, s_mx = {}, {}, {}, {}
    for u in range(NU):
        s_n[u] = u + 1 if u >= NU - TAIL_N else u + 2
        if u > 0:
            s_n[u] = max(s_n[u], s_n[u - 1])
        s_c[u] = s_n[u] + 1
        s_q[u] = s_c[u] + 1
        a, j0, nj = UNITS[u]
        s_mx[u] = s_q[u] + 1
        if a == 0:
            s_mx[u] = max(s_mx[u], X_STEP + 2 + (j0 + nj - 1) // XJ)
        if u > 0:
            s_mx[u] = max(s_mx[u], s_mx[u - 1])
        if u > 1:
            s_mx[u] = max(s_mx[u], s_mx[u - 2] + 1)
    return s_n, s_c, s_q, s_mx


def tile_learnablemasktemporalaggregation_kernel(tc, x, learnable_offset, predefined_weights, out):
    nc = tc.nc
    off_v = learnable_offset.rearrange("j (a p) m -> a p j m", p=P)
    pre_v = predefined_weights.rearrange("(a p) m -> p a m", p=P)
    x_v = x.rearrange("b (t p) j -> p (b t) j", p=P)
    out_v = out.rearrange("b (a p) j -> a p b j", p=P)
    s_n, s_c, s_q, s_mx = step_tables()

    with ExitStack() as ctx:
        const = ctx.enter_context(tc.tile_pool(name="const", bufs=1))
        ld = ctx.enter_context(tc.tile_pool(name="ld", bufs=PREFETCH + 1))
        zp = ctx.enter_context(tc.tile_pool(name="zp", bufs=5))
        st = ctx.enter_context(tc.tile_pool(name="st", bufs=8))
        mp = ctx.enter_context(tc.tile_pool(name="mp", bufs=3))
        gp = ctx.enter_context(tc.tile_pool(name="gp", bufs=3))
        cp = ctx.enter_context(tc.tile_pool(name="cp", bufs=9))
        op = ctx.enter_context(tc.tile_pool(name="op", bufs=2))
        psum_c = ctx.enter_context(tc.psum_pool(name="psum_c", bufs=1))
        psum_t = ctx.enter_context(tc.psum_pool(name="psum_t", bufs=4))
        psum_o = ctx.enter_context(tc.psum_pool(name="psum_o", bufs=2))
        ctx.enter_context(tc.manual_schedule())

        off_t, z_t, nmax_t, ssum_t, rinv_t, mask_t = {}, {}, {}, {}, {}, {}
        pt_t, grp_t, codes_t, scl_t, po_t, o_t = {}, {}, {}, {}, {}, {}

        ident = const.tile([P, P], BF16)
        make_identity(nc, ident[:])
        pre_sb = const.tile([P, NT, N], BF16)
        nc.sync.dma_start(out=pre_sb[:, 0:1, :], in_=pre_v[:, 0:1, :])
        pre_ps = [psum_c.tile([P, 2, N], BF16, name="pre_ps%d" % i) for i in range(2)]

        x_raw = const.tile([P, B * PACK, J], BF16)
        x_grp = const.tile([P, J, B * PACK], BF16, align_bytes=64)
        x_codes = const.tile([P, J * B], U32, align_bytes=64)
        x_scl = const.tile([P, J * B], U8, align_bytes=64)

        def x_load(c):
            nc.sync.dma_start(out=x_raw[:, 32 * c:32 * (c + 1), :], in_=x_v[:, 32 * c:32 * (c + 1), :])

        def x_group(c):
            nc.gpsimd.tensor_scalar(
                out=x_grp[:, XJ * c:XJ * (c + 1), :],
                in0=x_raw[:, :, XJ * c:XJ * (c + 1)].rearrange("p c j -> p j c"),
                scalar1=1.0, scalar2=0.0, op0=ALU.mult, op1=ALU.add,
            )

        def x_quant(c):
            w = XJ * B
            nc.vector.quantize_mx(
                out=x_codes[:, w * c:w * (c + 1)].bitcast(FP8X4),
                scales=x_scl[:, w * c:w * (c + 1)],
                in_=x_grp[:, XJ * c:XJ * (c + 1), :].rearrange("p j c -> p (j c)"),
            )

        def load(u):
            a, j0, nj = UNITS[u]
            off_t[u] = ld.tile([P, nj, N], BF16, name="off")
            nc.sync.dma_start(out=off_t[u][:], in_=off_v[a][:, j0:j0 + nj, :])

        def add(u):
            a, j0, nj = UNITS[u]
            z_t[u] = zp.tile([P, nj, N], F32, name="z")
            if u < SBUF_PRE_UNITS:
                pre_ap = pre_sb[:, a:a + 1, :]
            else:
                pre_ap = pre_ps[a // 2][:, a % 2:a % 2 + 1, :]
            nc.vector.tensor_tensor(
                out=z_t[u][:], in0=off_t[u][:], in1=pre_ap.to_broadcast([P, nj, N]), op=ALU.add,
            )

        def rowmax(u):
            a, j0, nj = UNITS[u]
            nmax_t[u] = st.tile([P, nj], F32, name="nmax")
            nc.vector.tensor_reduce(out=nmax_t[u][:], in_=z_t[u][:], axis=AX.X, op=ALU.max, negate=True)

        def exps(u):
            a, j0, nj = UNITS[u]
            ssum_t[u] = st.tile([P, nj], F32, name="ssum")
            for jj in range(nj):
                nc.scalar.activation(
                    out=z_t[u][:, jj, :], in_=z_t[u][:, jj, :], func=ACT.Exp,
                    bias=nmax_t[u][:, jj:jj + 1], scale=1.0, accum_out=ssum_t[u][:, jj:jj + 1],
                )

        def recip(u):
            a, j0, nj = UNITS[u]
            rinv_t[u] = st.tile([P, nj], F32, name="rinv")
            nc.vector.reciprocal(out=rinv_t[u][:], in_=ssum_t[u][:])

        def norm(u):
            a, j0, nj = UNITS[u]
            mask_t[u] = mp.tile([P, nj, N], BF16, name="mask")
            for jj in range(nj):
                if u >= NU - TAIL_N:
                    nc.vector.tensor_scalar(
                        out=mask_t[u][:, jj, :], in0=z_t[u][:, jj, :], scalar1=rinv_t[u][:, jj:jj + 1],
                        scalar2=None, op0=ALU.mult,
                    )
                else:
                    nc.gpsimd.tensor_scalar(
                        out=mask_t[u][:, jj, :], in0=z_t[u][:, jj, :], scalar1=rinv_t[u][:, jj:jj + 1],
                        scalar2=0.0, op0=ALU.mult, op1=ALU.add,
                    )

        def pieces(u):
            nj = UNITS[u][2]
            return [(q0, min(2, nj - q0)) for q0 in range(0, nj, 2)]

        def transp(u):
            pt_t[u] = []
            for q0, nq in pieces(u):
                pt = psum_t.tile([P, nq, PACK, P], BF16, name="pt")
                pt_t[u].append(pt)
                for q in range(nq):
                    for t in range(PACK):
                        nc.tensor.transpose(pt[:, q, t, :], mask_t[u][:, q0 + q, t * P:(t + 1) * P], ident[:])

        def copy_on_vector(u, i):
            return u >= NU - TAIL_C and (u + i) % 2 == 1

        def copy_out(u, on_vector):
            a, j0, nj = UNITS[u]
            if u not in grp_t:
                grp_t[u] = gp.tile([P, nj, P, PACK], BF16, name="grp", align_bytes=64)
            for i, (q0, nq) in enumerate(pieces(u)):
                if copy_on_vector(u, i) != on_vector:
                    continue
                dst = grp_t[u][:, q0:q0 + nq, :, :]
                src = pt_t[u][i][:].rearrange("p q t n -> p q n t")
                if on_vector:
                    nc.vector.tensor_copy(out=dst, in_=src)
                else:
                    nc.scalar.copy(out=dst, in_=src)

        def quant(u):
            a, j0, nj = UNITS[u]
            codes_t[u] = cp.tile([P, nj * P], U32, name="codes", align_bytes=64)
            scl_t[u] = cp.tile([P, nj * P], U8, name="scl", align_bytes=64)
            nc.vector.quantize_mx(
                out=codes_t[u][:].bitcast(FP8X4), scales=scl_t[u][:],
                in_=grp_t[u][:].rearrange("p j n t -> p (j n t)"),
            )

        def mx(u):
            a, j0, nj = UNITS[u]
            bank = (a, j0 // BANK_J)
            if j0 % BANK_J == 0:
                po_t[bank] = psum_o.tile([P, BANK_J, B], F32, name="po")
            for jj in range(nj):
                j = j0 + jj
                nc.tensor.matmul_mx(
                    out=po_t[bank][:, j % BANK_J, :],
                    lhsT=codes_t[u][:, jj * P:(jj + 1) * P].bitcast(FP8X4),
                    lhsT_scale=scl_t[u][:, jj * P:(jj + 1) * P],
                    rhs=x_codes[:, j * B:(j + 1) * B].bitcast(FP8X4),
                    rhs_scale=x_scl[:, j * B:(j + 1) * B],
                    start=True, stop=True,
                )

        def evac(u):
            a, j0, nj = UNITS[u]
            if (j0 + nj) % BANK_J != 0:
                return
            jb = j0 + nj - BANK_J
            if jb == 0:
                o_t[a] = op.tile([P, B, J], F32, name="o_sb")
            nc.scalar.copy(
                out=o_t[a][:, :, jb:jb + BANK_J], in_=po_t[(a, jb // BANK_J)][:].rearrange("p j b -> p b j"),
            )
            if jb + BANK_J == J:
                nc.sync.dma_start(out=out_v[a], in_=o_t[a][:])

        def at(table, k):
            return [u for u in range(NU) if table[u] == k]

        xl = 0
        for u in range(PREFETCH):
            load(u)
            if u == 0:
                nc.sync.dma_start(out=pre_sb[:, 1:NT, :], in_=pre_v[:, 1:NT, :])
            if u >= X_AFTER:
                x_load(xl)
                xl += 1
        for a in range(NT):
            nc.tensor.matmul(out=pre_ps[a // 2][:, a % 2, :], lhsT=ident[:], rhs=pre_sb[:, a, :], start=True, stop=True)
        for u in range(AHEAD):
            add(u)
        for k in range(max(s_mx[u] for u in range(NU)) + 2):
            if k + PREFETCH < NU:
                load(k + PREFETCH)
            if xl < 8:
                x_load(xl)
                xl += 1
            if 0 <= k - 1 < NU:
                exps(k - 1)
            for u in at(s_c, k):
                copy_out(u, False)
            for u in at(s_mx, k - 1):
                evac(u)
            for u in at(s_n, k):
                if u < NU - TAIL_N:
                    norm(u)
            if 0 <= k - X_STEP < 8:
                x_group(k - X_STEP)
            if k + AHEAD < NU:
                add(k + AHEAD)
            if k < NU:
                rowmax(k)
            for u in at(s_c, k):
                copy_out(u, True)
            if 0 <= k - 1 < NU:
                recip(k - 1)
            for u in at(s_q, k):
                quant(u)
            if 0 <= k - X_STEP - 1 < 8:
                x_quant(k - X_STEP - 1)
            for u in at(s_n, k):
                if u >= NU - TAIL_N:
                    norm(u)
            for u in at(s_n, k):
                transp(u)
            for u in at(s_mx, k):
                mx(u)
